import numpy as np
import ml_dtypes

BF16 = ml_dtypes.bfloat16


def bf(x):
    return np.asarray(x, np.float32).astype(BF16)


def f32(x):
    return np.asarray(x, np.float32)


def f64(x):
    return np.asarray(x).astype(np.float64)


def striped(idx):
    return np.tile(idx.reshape(-1, 16).T, (8, 1))


D, D3, S, KN, H, N = 256, 768, 512, 4, 256, 2048


def gelu_tanh(v):
    return 0.5 * v * (1.0 + np.tanh(np.sqrt(2.0 / np.pi) * (v + 0.044715 * v**3)))


def setup_inputs():
    r = np.random.standard_normal((D, S))
    r = r - r.mean(axis=0, keepdims=True)
    r = r / np.sqrt((r * r).mean(axis=0, keepdims=True))
    return {
        "x": f32(r),
        "e": bf(np.random.standard_normal((D, N))),
        "w1": bf(np.random.standard_normal((D3, D)) / np.sqrt(D3)),
        "b1": f32(0.1 * np.random.standard_normal((D, 1))),
        "w2": bf(np.random.standard_normal((D, D)) / np.sqrt(D)),
        "b2": f32(0.1 * np.random.standard_normal((D, 1))),
        "offs": striped(np.concatenate([np.random.permutation(S)[:H] for _ in range(N // H)])),
    }


def reference(x, e, w1, b1, w2, b2, offs):
    idx = offs[:16].T.reshape(-1)
    x = f64(x)
    vi = np.tile(x, (1, KN))
    vj = x[:, idx]
    cat = np.concatenate([vi, f64(e), vj], axis=0)
    hid = gelu_tanh(f64(w1).T @ cat + f64(b1))
    msg = f64(w2).T @ hid + f64(b2)
    return x + msg.reshape(D, KN, S).sum(axis=1) / KN

@@ -1,0 +1,113 @@
+import concourse.mybir as mybir
+
+F32, BF16, U16 = mybir.dt.float32, mybir.dt.bfloat16, mybir.dt.uint16
+COPY = mybir.ActivationFunctionType.Copy
+GELU_TANH = mybir.ActivationFunctionType.Gelu_apprx_tanh
+MULT, ADD = mybir.AluOpType.mult, mybir.AluOpType.add
+
+P = 128
+FEATURES = 256
+NODES = 512
+GROUPS = 4
+EDGES = GROUPS * NODES
+BLOCKS = FEATURES // P
+OFFSET_COLUMNS = NODES // 16
+
+FLOPS = 2 * (3 * FEATURES) * FEATURES * EDGES + 2 * FEATURES * FEATURES * EDGES
+
+
+def tile_sequencedenoiser_kernel(tc, x, e, w1, b1, w2, b2, offs, out):
+    nc = tc.nc
+    with (
+        tc.tile_pool(name="held", bufs=1) as held,
+        tc.psum_pool(name="hid_banks", bufs=6) as hid_banks,
+        tc.psum_pool(name="msg_banks", bufs=1) as msg_banks,
+    ):
+        offsets = held.tile([P, EDGES // 16], U16, name="offsets")
+        nc.sync.dma_start(offsets[:], offs)
+        x_f32 = [held.tile([P, NODES], F32, name=f"x_f32_{d}") for d in range(BLOCKS)]
+        for d in range(BLOCKS):
+            nc.sync.dma_start(x_f32[d][:], x[d * P : (d + 1) * P, :])
+        w1_sb = held.tile([P, 3 * BLOCKS, FEATURES], BF16, name="w1_sb")
+        nc.scalar.dma_start(w1_sb[:], w1.rearrange("(r p) m -> p r m", p=P))
+        e_sb = [held.tile([P, EDGES], BF16, name=f"e_sb_{d}") for d in range(BLOCKS)]
+        nc.sync.dma_start(e_sb[0][:], e[0:P, :])
+        nc.scalar.dma_start(e_sb[1][:], e[P : 2 * P, :])
+        w2_sb = held.tile([P, BLOCKS, FEATURES], BF16, name="w2_sb")
+        nc.scalar.dma_start(w2_sb[:], w2.rearrange("(r p) c -> p r c", p=P))
+        b1_sb = held.tile([P, BLOCKS], F32, name="b1_sb")
+        b2_sb = held.tile([P, BLOCKS], F32, name="b2_sb")
+        with nc.allow_non_contiguous_dma(reason="a bias lands one value to a partition"):
+            nc.gpsimd.dma_start(b1_sb[:], b1.rearrange("(r p) o -> p (r o)", p=P))
+            nc.gpsimd.dma_start(b2_sb[:], b2.rearrange("(r p) o -> p (r o)", p=P))
+
+        x_bf16 = [held.tile([P, NODES], BF16, name=f"x_bf16_{d}") for d in range(BLOCKS)]
+        x_plus_b2 = [held.tile([P, NODES], F32, name=f"x_plus_b2_{c}") for c in range(BLOCKS)]
+        for d in range(BLOCKS):
+            nc.vector.tensor_copy(x_bf16[d][:], x_f32[d][:])
+        for c in range(BLOCKS):
+            nc.vector.tensor_scalar_add(x_plus_b2[c][:], x_f32[c][:], b2_sb[:, c : c + 1])
+
+        msg_sum = [msg_banks.tile([P, NODES], F32, name=f"msg_sum_{c}") for c in range(BLOCKS)]
+
+        neighbours = {}
+        hid_sum = {}
+        hid = {}
+        for step in range(GROUPS + 2):
+            k = step
+            if k < GROUPS:
+                group_offsets = offsets[:, k * OFFSET_COLUMNS : (k + 1) * OFFSET_COLUMNS]
+                for d in range(BLOCKS):
+                    picked = held.tile([P, NODES], F32, name=f"picked_{k}_{d}")
+                    nc.scalar.activation(picked[:], x_f32[d][:].indirect(group_offsets), COPY)
+                    neighbours[k, d] = held.tile([P, NODES], BF16, name=f"neighbours_{k}_{d}")
+                    nc.vector.tensor_copy(neighbours[k, d][:], picked[:])
+                for m in range(BLOCKS):
+                    hid_sum[k, m] = hid_banks.tile([P, NODES], F32, name="hid_sum")
+                    for d in range(BLOCKS):
+                        nc.tensor.matmul(
+                            hid_sum[k, m][:],
+                            w1_sb[:, BLOCKS + d, m * P : (m + 1) * P],
+                            e_sb[d][:, k * NODES : (k + 1) * NODES],
+                            start=(d == 0),
+                            stop=False,
+                        )
+                    for d in range(BLOCKS):
+                        nc.tensor.matmul(
+                            hid_sum[k, m][:],
+                            w1_sb[:, d, m * P : (m + 1) * P],
+                            x_bf16[d][:],
+                            start=False,
+                            stop=False,
+                        )
+
+            k = step - 1
+            if 0 <= k < GROUPS:
+                for m in range(BLOCKS):
+                    for d in range(BLOCKS):
+                        nc.tensor.matmul(
+                            hid_sum[k, m][:],
+                            w1_sb[:, 2 * BLOCKS + d, m * P : (m + 1) * P],
+                            neighbours[k, d][:],
+                            start=False,
+                            stop=(d == BLOCKS - 1),
+                        )
+                    hid[k, m] = held.tile([P, NODES], BF16, name=f"hid_{k}_{m}")
+                    nc.scalar.activation(hid[k, m][:], hid_sum[k, m][:], GELU_TANH, bias=b1_sb[:, m : m + 1])
+
+            k = step - 2
+            if 0 <= k:
+                for c in range(BLOCKS):
+                    for m in range(BLOCKS):
+                        nc.tensor.matmul(
+                            msg_sum[c][:],
+                            w2_sb[:, m, c * P : (c + 1) * P],
+                            hid[k, m][:],
+                            start=(k == 0 and m == 0),
+                            stop=(k == GROUPS - 1 and m == BLOCKS - 1),
+                        )
+
+        for c in range(BLOCKS):
+            result = held.tile([P, NODES], F32, name=f"result_{c}")
+            nc.vector.scalar_tensor_tensor(result[:], msg_sum[c][:], 1.0 / GROUPS, x_plus_b2[c][:], MULT, ADD)
+            nc.sync.dma_start(out[c * P : (c + 1) * P, :], result[:])

@@ -20,40 +20,52 @@ def tile_sequencedenoiser_kernel(tc, x, e, w1, b1, w2, b2, offs, out):
     nc = tc.nc
     with (
         tc.tile_pool(name="held", bufs=1) as held,
-        tc.psum_pool(name="hid_banks", bufs=6) as hid_banks,
+        tc.psum_pool(name="first_banks", bufs=6) as first_banks,
         tc.psum_pool(name="msg_banks", bufs=1) as msg_banks,
     ):
         offsets = held.tile([P, EDGES // 16], U16, name="offsets")
-        nc.sync.dma_start(offsets[:], offs)
         x_f32 = [held.tile([P, NODES], F32, name=f"x_f32_{d}") for d in range(BLOCKS)]
-        for d in range(BLOCKS):
-            nc.sync.dma_start(x_f32[d][:], x[d * P : (d + 1) * P, :])
-        w1_sb = held.tile([P, 3 * BLOCKS, FEATURES], BF16, name="w1_sb")
-        nc.scalar.dma_start(w1_sb[:], w1.rearrange("(r p) m -> p r m", p=P))
         e_sb = [held.tile([P, EDGES], BF16, name=f"e_sb_{d}") for d in range(BLOCKS)]
-        nc.sync.dma_start(e_sb[0][:], e[0:P, :])
-        nc.scalar.dma_start(e_sb[1][:], e[P : 2 * P, :])
+        w1_sb = held.tile([P, 3 * BLOCKS, FEATURES], BF16, name="w1_sb")
+        w1_self, w1_edge, w1_neighbour = [w1_sb[:, t * BLOCKS : (t + 1) * BLOCKS, :] for t in range(3)]
         w2_sb = held.tile([P, BLOCKS, FEATURES], BF16, name="w2_sb")
-        nc.scalar.dma_start(w2_sb[:], w2.rearrange("(r p) c -> p r c", p=P))
         b1_sb = held.tile([P, BLOCKS], F32, name="b1_sb")
         b2_sb = held.tile([P, BLOCKS], F32, name="b2_sb")
+
+        nc.sync.dma_start(offsets[:], offs)
+        nc.scalar.dma_start(x_f32[0][:], x[0:P, :])
+        nc.sync.dma_start(x_f32[1][:], x[P : 2 * P, :])
+        nc.sync.dma_start(w1_sb[:], w1.rearrange("(r p) m -> p r m", p=P))
+        nc.scalar.dma_start(e_sb[0][:], e[0:P, :])
+        nc.sync.dma_start(e_sb[1][:], e[P : 2 * P, :])
+        nc.sync.dma_start(w2_sb[:], w2.rearrange("(r p) c -> p r c", p=P))
         with nc.allow_non_contiguous_dma(reason="a bias lands one value to a partition"):
             nc.gpsimd.dma_start(b1_sb[:], b1.rearrange("(r p) o -> p (r o)", p=P))
             nc.gpsimd.dma_start(b2_sb[:], b2.rearrange("(r p) o -> p (r o)", p=P))
 
+        table_warmer = held.tile([P, 1], F32, name="table_warmer")
+        nc.vector.memset(table_warmer[:], 0.0)
+        nc.scalar.activation(table_warmer[:], table_warmer[:], GELU_TANH)
+
         x_bf16 = [held.tile([P, NODES], BF16, name=f"x_bf16_{d}") for d in range(BLOCKS)]
-        x_plus_b2 = [held.tile([P, NODES], F32, name=f"x_plus_b2_{c}") for c in range(BLOCKS)]
         for d in range(BLOCKS):
             nc.vector.tensor_copy(x_bf16[d][:], x_f32[d][:])
-        for c in range(BLOCKS):
-            nc.vector.tensor_scalar_add(x_plus_b2[c][:], x_f32[c][:], b2_sb[:, c : c + 1])
-
-        msg_sum = [msg_banks.tile([P, NODES], F32, name=f"msg_sum_{c}") for c in range(BLOCKS)]
+        own_term = [held.tile([P, NODES], F32, name=f"own_term_{m}") for m in range(BLOCKS)]
+        for m in range(BLOCKS):
+            own_sum = first_banks.tile([P, NODES], F32, name="own_sum", tag="first_sum")
+            for d in range(BLOCKS):
+                nc.tensor.matmul(
+                    own_sum[:],
+                    w1_self[:, d, m * P : (m + 1) * P],
+                    x_bf16[d][:],
+                    start=(d == 0),
+                    stop=(d == BLOCKS - 1),
+                )
+            nc.vector.tensor_copy(own_term[m][:], own_sum[:])
 
         neighbours = {}
-        hid_sum = {}
-        hid = {}
-        for step in range(GROUPS + 2):
+        before_gelu = {}
+        for step in range(GROUPS + 1):
             k = step
             if k < GROUPS:
                 group_offsets = offsets[:, k * OFFSET_COLUMNS : (k + 1) * OFFSET_COLUMNS]
@@ -62,52 +74,49 @@ def tile_sequencedenoiser_kernel(tc, x, e, w1, b1, w2, b2, offs, out):
                     nc.scalar.activation(picked[:], x_f32[d][:].indirect(group_offsets), COPY)
                     neighbours[k, d] = held.tile([P, NODES], BF16, name=f"neighbours_{k}_{d}")
                     nc.vector.tensor_copy(neighbours[k, d][:], picked[:])
+
+            k = step - 1
+            if 0 <= k:
                 for m in range(BLOCKS):
-                    hid_sum[k, m] = hid_banks.tile([P, NODES], F32, name="hid_sum")
+                    pair_sum = first_banks.tile([P, NODES], F32, name="pair_sum", tag="first_sum")
                     for d in range(BLOCKS):
                         nc.tensor.matmul(
-                            hid_sum[k, m][:],
-                            w1_sb[:, BLOCKS + d, m * P : (m + 1) * P],
+                            pair_sum[:],
+                            w1_edge[:, d, m * P : (m + 1) * P],
                             e_sb[d][:, k * NODES : (k + 1) * NODES],
                             start=(d == 0),
                             stop=False,
                         )
                     for d in range(BLOCKS):
                         nc.tensor.matmul(
-                            hid_sum[k, m][:],
-                            w1_sb[:, d, m * P : (m + 1) * P],
-                            x_bf16[d][:],
-                            start=False,
-                            stop=False,
-                        )
-
-            k = step - 1
-            if 0 <= k < GROUPS:
-                for m in range(BLOCKS):
-                    for d in range(BLOCKS):
-                        nc.tensor.matmul(
-                            hid_sum[k, m][:],
-                            w1_sb[:, 2 * BLOCKS + d, m * P : (m + 1) * P],
+                            pair_sum[:],
+                            w1_neighbour[:, d, m * P : (m + 1) * P],
                             neighbours[k, d][:],
                             start=False,
                             stop=(d == BLOCKS - 1),
                         )
-                    hid[k, m] = held.tile([P, NODES], BF16, name=f"hid_{k}_{m}")
-                    nc.scalar.activation(hid[k, m][:], hid_sum[k, m][:], GELU_TANH, bias=b1_sb[:, m : m + 1])
+                    before_gelu[k, m] = held.tile([P, NODES], F32, name=f"before_gelu_{k}_{m}")
+                    nc.vector.tensor_add(before_gelu[k, m][:], pair_sum[:], own_term[m][:])
 
-            k = step - 2
-            if 0 <= k:
+        msg_sum = [msg_banks.tile([P, NODES], F32, name=f"msg_sum_{c}") for c in range(BLOCKS)]
+        for k in range(GROUPS):
+            for m in range(BLOCKS):
+                hid = held.tile([P, NODES], BF16, name=f"hid_{k}_{m}")
+                nc.scalar.activation(hid[:], before_gelu[k, m][:], GELU_TANH, bias=b1_sb[:, m : m + 1])
                 for c in range(BLOCKS):
-                    for m in range(BLOCKS):
-                        nc.tensor.matmul(
-                            msg_sum[c][:],
-                            w2_sb[:, m, c * P : (c + 1) * P],
-                            hid[k, m][:],
-                            start=(k == 0 and m == 0),
-                            stop=(k == GROUPS - 1 and m == BLOCKS - 1),
-                        )
+                    nc.tensor.matmul(
+                        msg_sum[c][:],
+                        w2_sb[:, m, c * P : (c + 1) * P],
+                        hid[:],
+                        start=(k == 0 and m == 0),
+                        stop=(k == GROUPS - 1 and m == BLOCKS - 1),
+                    )
 
+        x_plus_b2 = [held.tile([P, NODES], F32, name=f"x_plus_b2_{c}") for c in range(BLOCKS)]
+        for c in range(BLOCKS):
+            nc.vector.tensor_scalar_add(x_plus_b2[c][:], x_f32[c][:], b2_sb[:, c : c + 1])
+        store_queue = [nc.sync, nc.scalar]
         for c in range(BLOCKS):
             result = held.tile([P, NODES], F32, name=f"result_{c}")
             nc.vector.scalar_tensor_tensor(result[:], msg_sum[c][:], 1.0 / GROUPS, x_plus_b2[c][:], MULT, ADD)
-            nc.sync.dma_start(out[c * P : (c + 1) * P, :], result[:])
+            store_queue[c].dma_start(out[c * P : (c + 1) * P, :], result[:])

@@ -20,24 +20,31 @@ def tile_sequencedenoiser_kernel(tc, x, e, w1, b1, w2, b2, offs, out):
     nc = tc.nc
     with (
         tc.tile_pool(name="held", bufs=1) as held,
-        tc.psum_pool(name="first_banks", bufs=6) as first_banks,
+        tc.psum_pool(name="pair_banks", bufs=6) as pair_banks,
         tc.psum_pool(name="msg_banks", bufs=1) as msg_banks,
     ):
         offsets = held.tile([P, EDGES // 16], U16, name="offsets")
         x_f32 = [held.tile([P, NODES], F32, name=f"x_f32_{d}") for d in range(BLOCKS)]
-        e_sb = [held.tile([P, EDGES], BF16, name=f"e_sb_{d}") for d in range(BLOCKS)]
-        w1_sb = held.tile([P, 3 * BLOCKS, FEATURES], BF16, name="w1_sb")
-        w1_self, w1_edge, w1_neighbour = [w1_sb[:, t * BLOCKS : (t + 1) * BLOCKS, :] for t in range(3)]
+        e_sb = [held.tile([P, BLOCKS, NODES], BF16, name=f"e_sb_{k}") for k in range(GROUPS)]
+        e_groups = [e[:, k * NODES : (k + 1) * NODES].rearrange("(d p) j -> p d j", p=P) for k in range(GROUPS)]
+        w1_self = held.tile([P, BLOCKS, FEATURES], BF16, name="w1_self")
+        w1_edge = held.tile([P, BLOCKS, FEATURES], BF16, name="w1_edge")
+        w1_neighbour = held.tile([P, BLOCKS, FEATURES], BF16, name="w1_neighbour")
+        w1_thirds = [w1[t * FEATURES : (t + 1) * FEATURES, :].rearrange("(d p) m -> p d m", p=P) for t in range(3)]
         w2_sb = held.tile([P, BLOCKS, FEATURES], BF16, name="w2_sb")
         b1_sb = held.tile([P, BLOCKS], F32, name="b1_sb")
         b2_sb = held.tile([P, BLOCKS], F32, name="b2_sb")
 
+        nc.sync.dma_start(w1_edge[:], w1_thirds[1])
+        nc.scalar.dma_start(e_sb[0][:], e_groups[0])
         nc.sync.dma_start(offsets[:], offs)
         nc.scalar.dma_start(x_f32[0][:], x[0:P, :])
         nc.sync.dma_start(x_f32[1][:], x[P : 2 * P, :])
-        nc.sync.dma_start(w1_sb[:], w1.rearrange("(r p) m -> p r m", p=P))
-        nc.scalar.dma_start(e_sb[0][:], e[0:P, :])
-        nc.sync.dma_start(e_sb[1][:], e[P : 2 * P, :])
+        nc.scalar.dma_start(e_sb[1][:], e_groups[1])
+        nc.sync.dma_start(w1_self[:], w1_thirds[0])
+        nc.sync.dma_start(w1_neighbour[:], w1_thirds[2])
+        nc.sync.dma_start(e_sb[2][:], e_groups[2])
+        nc.sync.dma_start(e_sb[3][:], e_groups[3])
         nc.sync.dma_start(w2_sb[:], w2.rearrange("(r p) c -> p r c", p=P))
         with nc.allow_non_contiguous_dma(reason="a bias lands one value to a partition"):
             nc.gpsimd.dma_start(b1_sb[:], b1.rearrange("(r p) o -> p (r o)", p=P))
@@ -51,23 +58,37 @@ def tile_sequencedenoiser_kernel(tc, x, e, w1, b1, w2, b2, offs, out):
         for d in range(BLOCKS):
             nc.vector.tensor_copy(x_bf16[d][:], x_f32[d][:])
         own_term = [held.tile([P, NODES], F32, name=f"own_term_{m}") for m in range(BLOCKS)]
-        for m in range(BLOCKS):
-            own_sum = first_banks.tile([P, NODES], F32, name="own_sum", tag="first_sum")
-            for d in range(BLOCKS):
-                nc.tensor.matmul(
-                    own_sum[:],
-                    w1_self[:, d, m * P : (m + 1) * P],
-                    x_bf16[d][:],
-                    start=(d == 0),
-                    stop=(d == BLOCKS - 1),
-                )
-            nc.vector.tensor_copy(own_term[m][:], own_sum[:])
-
         neighbours = {}
+        pair_sum = {}
         before_gelu = {}
-        for step in range(GROUPS + 1):
+        for step in range(GROUPS + 2):
+            k = step - 2
+            if 0 <= k:
+                for d in range(BLOCKS):
+                    for m in range(BLOCKS):
+                        nc.tensor.matmul(
+                            pair_sum[k, m][:],
+                            w1_neighbour[:, d, m * P : (m + 1) * P],
+                            neighbours[k, d][:],
+                            start=False,
+                            stop=(d == BLOCKS - 1),
+                        )
+                for m in range(BLOCKS):
+                    before_gelu[k, m] = held.tile([P, NODES], F32, name=f"before_gelu_{k}_{m}")
+                    nc.vector.tensor_add(before_gelu[k, m][:], pair_sum[k, m][:], own_term[m][:])
+
             k = step
             if k < GROUPS:
+                for m in range(BLOCKS):
+                    pair_sum[k, m] = pair_banks.tile([P, NODES], F32, name="pair_sum")
+                    for d in range(BLOCKS):
+                        nc.tensor.matmul(
+                            pair_sum[k, m][:],
+                            w1_edge[:, d, m * P : (m + 1) * P],
+                            e_sb[k][:, d, :],
+                            start=(d == 0),
+                            stop=False,
+                        )
                 group_offsets = offsets[:, k * OFFSET_COLUMNS : (k + 1) * OFFSET_COLUMNS]
                 for d in range(BLOCKS):
                     picked = held.tile([P, NODES], F32, name=f"picked_{k}_{d}")
@@ -75,28 +96,18 @@ def tile_sequencedenoiser_kernel(tc, x, e, w1, b1, w2, b2, offs, out):
                     neighbours[k, d] = held.tile([P, NODES], BF16, name=f"neighbours_{k}_{d}")
                     nc.vector.tensor_copy(neighbours[k, d][:], picked[:])
 
-            k = step - 1
-            if 0 <= k:
+            if step == 0:
                 for m in range(BLOCKS):
-                    pair_sum = first_banks.tile([P, NODES], F32, name="pair_sum", tag="first_sum")
+                    own_sum = msg_banks.tile([P, NODES], F32, name="own_sum", tag=f"msg_sum_{m}")
                     for d in range(BLOCKS):
                         nc.tensor.matmul(
-                            pair_sum[:],
-                            w1_edge[:, d, m * P : (m + 1) * P],
-                            e_sb[d][:, k * NODES : (k + 1) * NODES],
+                            own_sum[:],
+                            w1_self[:, d, m * P : (m + 1) * P],
+                            x_bf16[d][:],
                             start=(d == 0),
-                            stop=False,
-                        )
-                    for d in range(BLOCKS):
-                        nc.tensor.matmul(
-                            pair_sum[:],
-                            w1_neighbour[:, d, m * P : (m + 1) * P],
-                            neighbours[k, d][:],
-                            start=False,
                             stop=(d == BLOCKS - 1),
                         )
-                    before_gelu[k, m] = held.tile([P, NODES], F32, name=f"before_gelu_{k}_{m}")
-                    nc.vector.tensor_add(before_gelu[k, m][:], pair_sum[:], own_term[m][:])
+                    nc.vector.tensor_copy(own_term[m][:], own_sum[:])
 
         msg_sum = [msg_banks.tile([P, NODES], F32, name=f"msg_sum_{c}") for c in range(BLOCKS)]
         for k in range(GROUPS):

@@ -12,6 +12,7 @@ GROUPS = 4
 EDGES = GROUPS * NODES
 BLOCKS = FEATURES // P
 OFFSET_COLUMNS = NODES // 16
+WARMING_MATMULS = 4
 
 FLOPS = 2 * (3 * FEATURES) * FEATURES * EDGES + 2 * FEATURES * FEATURES * EDGES
 
@@ -49,6 +50,12 @@ def tile_sequencedenoiser_kernel(tc, x, e, w1, b1, w2, b2, offs, out):
         with nc.allow_non_contiguous_dma(reason="a bias lands one value to a partition"):
             nc.gpsimd.dma_start(b1_sb[:], b1.rearrange("(r p) o -> p (r o)", p=P))
             nc.gpsimd.dma_start(b2_sb[:], b2.rearrange("(r p) o -> p (r o)", p=P))
+
+        zeros = held.tile([P, NODES], BF16, name="zeros")
+        nc.vector.memset(zeros[:], 0.0)
+        unread_product = msg_banks.tile([P, NODES], F32, name="unread_product", tag="msg_sum_0")
+        for repeat in range(WARMING_MATMULS):
+            nc.tensor.matmul(unread_product[:], zeros[:, 0:P], zeros[:], start=True, stop=True)
 
         table_warmer = held.tile([P, 1], F32, name="table_warmer")
         nc.vector.memset(table_warmer[:], 0.0)
@@ -96,7 +103,7 @@ def tile_sequencedenoiser_kernel(tc, x, e, w1, b1, w2, b2, offs, out):
                     neighbours[k, d] = held.tile([P, NODES], BF16, name=f"neighbours_{k}_{d}")
                     nc.vector.tensor_copy(neighbours[k, d][:], picked[:])
 
-            if step == 0:
+            if step == 1:
                 for m in range(BLOCKS):
                     own_sum = msg_banks.tile([P, NODES], F32, name="own_sum", tag=f"msg_sum_{m}")
                     for d in range(BLOCKS):

@@ -12,7 +12,6 @@ GROUPS = 4
 EDGES = GROUPS * NODES
 BLOCKS = FEATURES // P
 OFFSET_COLUMNS = NODES // 16
-WARMING_MATMULS = 4
 
 FLOPS = 2 * (3 * FEATURES) * FEATURES * EDGES + 2 * FEATURES * FEATURES * EDGES
 
@@ -50,12 +49,6 @@ def tile_sequencedenoiser_kernel(tc, x, e, w1, b1, w2, b2, offs, out):
         with nc.allow_non_contiguous_dma(reason="a bias lands one value to a partition"):
             nc.gpsimd.dma_start(b1_sb[:], b1.rearrange("(r p) o -> p (r o)", p=P))
             nc.gpsimd.dma_start(b2_sb[:], b2.rearrange("(r p) o -> p (r o)", p=P))
-
-        zeros = held.tile([P, NODES], BF16, name="zeros")
-        nc.vector.memset(zeros[:], 0.0)
-        unread_product = msg_banks.tile([P, NODES], F32, name="unread_product", tag="msg_sum_0")
-        for repeat in range(WARMING_MATMULS):
-            nc.tensor.matmul(unread_product[:], zeros[:, 0:P], zeros[:], start=True, stop=True)
 
         table_warmer = held.tile([P, 1], F32, name="table_warmer")
         nc.vector.memset(table_warmer[:], 0.0)

@@ -96,7 +96,7 @@ def tile_sequencedenoiser_kernel(tc, x, e, w1, b1, w2, b2, offs, out):
                     neighbours[k, d] = held.tile([P, NODES], BF16, name=f"neighbours_{k}_{d}")
                     nc.vector.tensor_copy(neighbours[k, d][:], picked[:])
 
-            if step == 1:
+            if step == 0:
                 for m in range(BLOCKS):
                     own_sum = msg_banks.tile([P, NODES], F32, name="own_sum", tag=f"msg_sum_{m}")
                     for d in range(BLOCKS):
@@ -129,5 +129,9 @@ def tile_sequencedenoiser_kernel(tc, x, e, w1, b1, w2, b2, offs, out):
         store_queue = [nc.sync, nc.scalar]
         for c in range(BLOCKS):
             result = held.tile([P, NODES], F32, name=f"result_{c}")
-            nc.vector.scalar_tensor_tensor(result[:], msg_sum[c][:], 1.0 / GROUPS, x_plus_b2[c][:], MULT, ADD)
-            store_queue[c].dma_start(out[c * P : (c + 1) * P, :], result[:])
+            for h in range(2):
+                half = slice(h * (NODES // 2), (h + 1) * (NODES // 2))
+                nc.vector.scalar_tensor_tensor(
+                    result[:, half], msg_sum[c][:, half], 1.0 / GROUPS, x_plus_b2[c][:, half], MULT, ADD
+                )
+                store_queue[h].dma_start(out[c * P : (c + 1) * P, half], result[:, half])

@@ -35,13 +35,13 @@ def tile_sequencedenoiser_kernel(tc, x, e, w1, b1, w2, b2, offs, out):
         b1_sb = held.tile([P, BLOCKS], F32, name="b1_sb")
         b2_sb = held.tile([P, BLOCKS], F32, name="b2_sb")
 
-        nc.sync.dma_start(w1_edge[:], w1_thirds[1])
-        nc.scalar.dma_start(e_sb[0][:], e_groups[0])
         nc.sync.dma_start(offsets[:], offs)
-        nc.scalar.dma_start(x_f32[0][:], x[0:P, :])
-        nc.sync.dma_start(x_f32[1][:], x[P : 2 * P, :])
-        nc.scalar.dma_start(e_sb[1][:], e_groups[1])
-        nc.sync.dma_start(w1_self[:], w1_thirds[0])
+        for d in range(BLOCKS):
+            nc.scalar.dma_start(x_f32[d][:], x[d * P : (d + 1) * P, :])
+        nc.sync.dma_start(w1_edge[:], w1_thirds[1])
+        nc.sync.dma_start(e_sb[0][:], e_groups[0])
+        nc.sync.dma_start(e_sb[1][:], e_groups[1])
+        nc.scalar.dma_start(w1_self[:], w1_thirds[0])
         nc.sync.dma_start(w1_neighbour[:], w1_thirds[2])
         nc.sync.dma_start(e_sb[2][:], e_groups[2])
         nc.sync.dma_start(e_sb[3][:], e_groups[3])
@@ -96,7 +96,7 @@ def tile_sequencedenoiser_kernel(tc, x, e, w1, b1, w2, b2, offs, out):
                     neighbours[k, d] = held.tile([P, NODES], BF16, name=f"neighbours_{k}_{d}")
                     nc.vector.tensor_copy(neighbours[k, d][:], picked[:])
 
-            if step == 0:
+            if step == 1:
                 for m in range(BLOCKS):
                     own_sum = msg_banks.tile([P, NODES], F32, name="own_sum", tag=f"msg_sum_{m}")
                     for d in range(BLOCKS):

@@ -110,7 +110,7 @@ def tile_sequencedenoiser_kernel(tc, x, e, w1, b1, w2, b2, offs, out):
                     nc.vector.tensor_copy(own_term[m][:], own_sum[:])
 
         msg_sum = [msg_banks.tile([P, NODES], F32, name=f"msg_sum_{c}") for c in range(BLOCKS)]
-        for k in range(GROUPS):
+        for k in range(GROUPS - 1):
             for m in range(BLOCKS):
                 hid = held.tile([P, NODES], BF16, name=f"hid_{k}_{m}")
                 nc.scalar.activation(hid[:], before_gelu[k, m][:], GELU_TANH, bias=b1_sb[:, m : m + 1])
@@ -120,18 +120,34 @@ def tile_sequencedenoiser_kernel(tc, x, e, w1, b1, w2, b2, offs, out):
                         w2_sb[:, m, c * P : (c + 1) * P],
                         hid[:],
                         start=(k == 0 and m == 0),
-                        stop=(k == GROUPS - 1 and m == BLOCKS - 1),
+                        stop=(k == GROUPS - 2 and m == BLOCKS - 1),
                     )
 
         x_plus_b2 = [held.tile([P, NODES], F32, name=f"x_plus_b2_{c}") for c in range(BLOCKS)]
+        without_last = [held.tile([P, NODES], F32, name=f"without_last_{c}") for c in range(BLOCKS)]
         for c in range(BLOCKS):
             nc.vector.tensor_scalar_add(x_plus_b2[c][:], x_f32[c][:], b2_sb[:, c : c + 1])
+            nc.vector.scalar_tensor_tensor(without_last[c][:], msg_sum[c][:], 1.0 / GROUPS, x_plus_b2[c][:], MULT, ADD)
+
+        k = GROUPS - 1
         store_queue = [nc.sync, nc.scalar]
-        for c in range(BLOCKS):
-            result = held.tile([P, NODES], F32, name=f"result_{c}")
-            for h in range(2):
-                half = slice(h * (NODES // 2), (h + 1) * (NODES // 2))
+        result = [held.tile([P, NODES], F32, name=f"result_{c}") for c in range(BLOCKS)]
+        for h in range(2):
+            half = slice(h * (NODES // 2), (h + 1) * (NODES // 2))
+            last_sum = [pair_banks.tile([P, NODES // 2], F32, name=f"last_sum_{c}", tag="pair_sum") for c in range(BLOCKS)]
+            for m in range(BLOCKS):
+                hid = held.tile([P, NODES // 2], BF16, name=f"hid_{k}_{m}_{h}")
+                nc.scalar.activation(hid[:], before_gelu[k, m][:, half], GELU_TANH, bias=b1_sb[:, m : m + 1])
+                for c in range(BLOCKS):
+                    nc.tensor.matmul(
+                        last_sum[c][:],
+                        w2_sb[:, m, c * P : (c + 1) * P],
+                        hid[:],
+                        start=(m == 0),
+                        stop=(m == BLOCKS - 1),
+                    )
+            for c in range(BLOCKS):
                 nc.vector.scalar_tensor_tensor(
-                    result[:, half], msg_sum[c][:, half], 1.0 / GROUPS, x_plus_b2[c][:, half], MULT, ADD
+                    result[c][:, half], last_sum[c][:], 1.0 / GROUPS, without_last[c][:, half], MULT, ADD
                 )
-                store_queue[h].dma_start(out[c * P : (c + 1) * P, half], result[:, half])
+                store_queue[c].dma_start(out[c * P : (c + 1) * P, half], result[c][:, half])

@@ -35,13 +35,13 @@ def tile_sequencedenoiser_kernel(tc, x, e, w1, b1, w2, b2, offs, out):
         b1_sb = held.tile([P, BLOCKS], F32, name="b1_sb")
         b2_sb = held.tile([P, BLOCKS], F32, name="b2_sb")
 
-        nc.sync.dma_start(offsets[:], offs)
-        for d in range(BLOCKS):
-            nc.scalar.dma_start(x_f32[d][:], x[d * P : (d + 1) * P, :])
-        nc.sync.dma_start(w1_edge[:], w1_thirds[1])
         nc.sync.dma_start(e_sb[0][:], e_groups[0])
+        nc.scalar.dma_start(w1_edge[:], w1_thirds[1])
+        nc.sync.dma_start(offsets[:], offs)
+        nc.scalar.dma_start(x_f32[0][:], x[0:P, :])
+        nc.gpsimd.dma_start(w1_self[:], w1_thirds[0])
+        nc.sync.dma_start(x_f32[1][:], x[P : 2 * P, :])
         nc.sync.dma_start(e_sb[1][:], e_groups[1])
-        nc.scalar.dma_start(w1_self[:], w1_thirds[0])
         nc.sync.dma_start(w1_neighbour[:], w1_thirds[2])
         nc.sync.dma_start(e_sb[2][:], e_groups[2])
         nc.sync.dma_start(e_sb[3][:], e_groups[3])

@@ -81,7 +81,8 @@ def tile_sequencedenoiser_kernel(tc, x, e, w1, b1, w2, b2, offs, out):
             if k < GROUPS:
                 for m in range(BLOCKS):
                     pair_sum[k, m] = pair_banks.tile([P, NODES], F32, name="pair_sum")
-                    for d in range(BLOCKS):
+                for d in range(BLOCKS):
+                    for m in range(BLOCKS):
                         nc.tensor.matmul(
                             pair_sum[k, m][:],
                             w1_edge[:, d, m * P : (m + 1) * P],
@@ -109,45 +110,56 @@ def tile_sequencedenoiser_kernel(tc, x, e, w1, b1, w2, b2, offs, out):
                         )
                     nc.vector.tensor_copy(own_term[m][:], own_sum[:])
 
-        msg_sum = [msg_banks.tile([P, NODES], F32, name=f"msg_sum_{c}") for c in range(BLOCKS)]
-        for k in range(GROUPS - 1):
+        HALF = NODES // 2
+        halves = [slice(h * HALF, (h + 1) * HALF) for h in range(2)]
+        x_plus_b2 = [held.tile([P, NODES], F32, name=f"x_plus_b2_{c}") for c in range(BLOCKS)]
+        for c in range(BLOCKS):
+            nc.vector.tensor_scalar_add(x_plus_b2[c][:], x_f32[c][:], b2_sb[:, c : c + 1])
+
+        early_sum = [msg_banks.tile([P, NODES], F32, name=f"msg_sum_{c}") for c in range(BLOCKS)]
+        for k in range(2):
             for m in range(BLOCKS):
                 hid = held.tile([P, NODES], BF16, name=f"hid_{k}_{m}")
                 nc.scalar.activation(hid[:], before_gelu[k, m][:], GELU_TANH, bias=b1_sb[:, m : m + 1])
                 for c in range(BLOCKS):
                     nc.tensor.matmul(
-                        msg_sum[c][:],
+                        early_sum[c][:],
                         w2_sb[:, m, c * P : (c + 1) * P],
                         hid[:],
                         start=(k == 0 and m == 0),
-                        stop=(k == GROUPS - 2 and m == BLOCKS - 1),
+                        stop=(k == 1 and m == BLOCKS - 1),
+                    )
+        without_late = [held.tile([P, NODES], F32, name=f"without_late_{c}") for c in range(BLOCKS)]
+        for c in range(BLOCKS):
+            nc.vector.scalar_tensor_tensor(without_late[c][:], early_sum[c][:], 1.0 / GROUPS, x_plus_b2[c][:], MULT, ADD)
+
+        late_sum = {
+            (c, h): pair_banks.tile([P, HALF], F32, name=f"late_sum_{c}_{h}", tag="pair_sum")
+            for h in range(2)
+            for c in range(BLOCKS)
+        }
+        for m in range(BLOCKS):
+            hid = held.tile([P, NODES], BF16, name=f"hid_2_{m}")
+            nc.scalar.activation(hid[:], before_gelu[2, m][:], GELU_TANH, bias=b1_sb[:, m : m + 1])
+            for h in range(2):
+                for c in range(BLOCKS):
+                    nc.tensor.matmul(
+                        late_sum[c, h][:], w2_sb[:, m, c * P : (c + 1) * P], hid[:, halves[h]], start=(m == 0), stop=False
                     )
 
-        x_plus_b2 = [held.tile([P, NODES], F32, name=f"x_plus_b2_{c}") for c in range(BLOCKS)]
-        without_last = [held.tile([P, NODES], F32, name=f"without_last_{c}") for c in range(BLOCKS)]
-        for c in range(BLOCKS):
-            nc.vector.tensor_scalar_add(x_plus_b2[c][:], x_f32[c][:], b2_sb[:, c : c + 1])
-            nc.vector.scalar_tensor_tensor(without_last[c][:], msg_sum[c][:], 1.0 / GROUPS, x_plus_b2[c][:], MULT, ADD)
-
-        k = GROUPS - 1
         store_queue = [nc.sync, nc.scalar]
         result = [held.tile([P, NODES], F32, name=f"result_{c}") for c in range(BLOCKS)]
         for h in range(2):
-            half = slice(h * (NODES // 2), (h + 1) * (NODES // 2))
-            last_sum = [pair_banks.tile([P, NODES // 2], F32, name=f"last_sum_{c}", tag="pair_sum") for c in range(BLOCKS)]
+            last_hid = []
             for m in range(BLOCKS):
-                hid = held.tile([P, NODES // 2], BF16, name=f"hid_{k}_{m}_{h}")
-                nc.scalar.activation(hid[:], before_gelu[k, m][:, half], GELU_TANH, bias=b1_sb[:, m : m + 1])
-                for c in range(BLOCKS):
-                    nc.tensor.matmul(
-                        last_sum[c][:],
-                        w2_sb[:, m, c * P : (c + 1) * P],
-                        hid[:],
-                        start=(m == 0),
-                        stop=(m == BLOCKS - 1),
-                    )
+                last_hid.append(held.tile([P, HALF], BF16, name=f"hid_3_{m}_{h}"))
+                nc.scalar.activation(last_hid[m][:], before_gelu[3, m][:, halves[h]], GELU_TANH, bias=b1_sb[:, m : m + 1])
             for c in range(BLOCKS):
+                for m in range(BLOCKS):
+                    nc.tensor.matmul(
+                        late_sum[c, h][:], w2_sb[:, m, c * P : (c + 1) * P], last_hid[m][:], start=False, stop=(m == BLOCKS - 1)
+                    )
                 nc.vector.scalar_tensor_tensor(
-                    result[c][:, half], last_sum[c][:], 1.0 / GROUPS, without_last[c][:, half], MULT, ADD
+                    result[c][:, halves[h]], late_sum[c, h][:], 1.0 / GROUPS, without_late[c][:, halves[h]], MULT, ADD
                 )
-                store_queue[c].dma_start(out[c * P : (c + 1) * P, half], result[c][:, half])
+                store_queue[c].dma_start(out[c * P : (c + 1) * P, halves[h]], result[c][:, halves[h]])

@@ -11,7 +11,7 @@ NODES = 512
 GROUPS = 4
 EDGES = GROUPS * NODES
 BLOCKS = FEATURES // P
-OFFSET_COLUMNS = NODES // 16
+PIECE = 256
 
 FLOPS = 2 * (3 * FEATURES) * FEATURES * EDGES + 2 * FEATURES * FEATURES * EDGES
 
@@ -69,7 +69,7 @@ def tile_sequencedenoiser_kernel(tc, x, e, w1, b1, w2, b2, offs, out):
                         nc.tensor.matmul(
                             pair_sum[k, m][:],
                             w1_neighbour[:, d, m * P : (m + 1) * P],
-                            neighbours[k, d][:],
+                            neighbours[k][:, :, d],
                             start=False,
                             stop=(d == BLOCKS - 1),
                         )
@@ -90,12 +90,15 @@ def tile_sequencedenoiser_kernel(tc, x, e, w1, b1, w2, b2, offs, out):
                             start=(d == 0),
                             stop=False,
                         )
-                group_offsets = offsets[:, k * OFFSET_COLUMNS : (k + 1) * OFFSET_COLUMNS]
+                neighbours[k] = held.tile([P, NODES, BLOCKS], BF16, name=f"neighbours_{k}")
                 for d in range(BLOCKS):
-                    picked = held.tile([P, NODES], F32, name=f"picked_{k}_{d}")
-                    nc.scalar.activation(picked[:], x_f32[d][:].indirect(group_offsets), COPY)
-                    neighbours[k, d] = held.tile([P, NODES], BF16, name=f"neighbours_{k}_{d}")
-                    nc.vector.tensor_copy(neighbours[k, d][:], picked[:])
+                    for piece in range(NODES // PIECE):
+                        first_column = (k * NODES + piece * PIECE) // 16
+                        nc.scalar.activation(
+                            neighbours[k][:, piece * PIECE : (piece + 1) * PIECE, d],
+                            x_bf16[d][:].indirect(offsets[:, first_column : first_column + PIECE // 16]),
+                            COPY,
+                        )
 
             if step == 1:
                 for m in range(BLOCKS):

@@ -91,14 +91,20 @@ def tile_sequencedenoiser_kernel(tc, x, e, w1, b1, w2, b2, offs, out):
                             stop=False,
                         )
                 neighbours[k] = held.tile([P, NODES, BLOCKS], BF16, name=f"neighbours_{k}")
-                for d in range(BLOCKS):
-                    for piece in range(NODES // PIECE):
-                        first_column = (k * NODES + piece * PIECE) // 16
-                        nc.scalar.activation(
-                            neighbours[k][:, piece * PIECE : (piece + 1) * PIECE, d],
-                            x_bf16[d][:].indirect(offsets[:, first_column : first_column + PIECE // 16]),
-                            COPY,
-                        )
+                if k == 0:
+                    for d in range(BLOCKS):
+                        picked = held.tile([P, NODES], F32, name=f"picked_{d}")
+                        nc.scalar.activation(picked[:], x_f32[d][:].indirect(offsets[:, 0 : NODES // 16]), COPY)
+                        nc.vector.tensor_copy(neighbours[k][:, :, d], picked[:])
+                else:
+                    for d in range(BLOCKS):
+                        for piece in range(NODES // PIECE):
+                            first_column = (k * NODES + piece * PIECE) // 16
+                            nc.scalar.activation(
+                                neighbours[k][:, piece * PIECE : (piece + 1) * PIECE, d],
+                                x_bf16[d][:].indirect(offsets[:, first_column : first_column + PIECE // 16]),
+                                COPY,
+                            )
 
             if step == 1:
                 for m in range(BLOCKS):

@@ -57,67 +57,66 @@ def tile_sequencedenoiser_kernel(tc, x, e, w1, b1, w2, b2, offs, out):
         x_bf16 = [held.tile([P, NODES], BF16, name=f"x_bf16_{d}") for d in range(BLOCKS)]
         for d in range(BLOCKS):
             nc.vector.tensor_copy(x_bf16[d][:], x_f32[d][:])
+        neighbours = [held.tile([P, NODES, BLOCKS], BF16, name=f"neighbours_{k}") for k in range(GROUPS)]
+        for d in range(BLOCKS):
+            picked = held.tile([P, NODES], F32, name=f"picked_{d}")
+            nc.scalar.activation(picked[:], x_f32[d][:].indirect(offsets[:, 0 : NODES // 16]), COPY)
+            nc.vector.tensor_copy(neighbours[0][:, :, d], picked[:])
+        for k in range(1, GROUPS):
+            for d in range(BLOCKS):
+                for piece in range(NODES // PIECE):
+                    first_column = (k * NODES + piece * PIECE) // 16
+                    nc.scalar.activation(
+                        neighbours[k][:, piece * PIECE : (piece + 1) * PIECE, d],
+                        x_bf16[d][:].indirect(offsets[:, first_column : first_column + PIECE // 16]),
+                        COPY,
+                    )
+
         own_term = [held.tile([P, NODES], F32, name=f"own_term_{m}") for m in range(BLOCKS)]
-        neighbours = {}
         pair_sum = {}
         before_gelu = {}
-        for step in range(GROUPS + 2):
-            k = step - 2
-            if 0 <= k:
-                for d in range(BLOCKS):
-                    for m in range(BLOCKS):
-                        nc.tensor.matmul(
-                            pair_sum[k, m][:],
-                            w1_neighbour[:, d, m * P : (m + 1) * P],
-                            neighbours[k][:, :, d],
-                            start=False,
-                            stop=(d == BLOCKS - 1),
-                        )
-                for m in range(BLOCKS):
-                    before_gelu[k, m] = held.tile([P, NODES], F32, name=f"before_gelu_{k}_{m}")
-                    nc.vector.tensor_add(before_gelu[k, m][:], pair_sum[k, m][:], own_term[m][:])
 
-            k = step
-            if k < GROUPS:
+        def edge_matmuls(k):
+            for m in range(BLOCKS):
+                pair_sum[k, m] = pair_banks.tile([P, NODES], F32, name="pair_sum")
+            for d in range(BLOCKS):
                 for m in range(BLOCKS):
-                    pair_sum[k, m] = pair_banks.tile([P, NODES], F32, name="pair_sum")
-                for d in range(BLOCKS):
-                    for m in range(BLOCKS):
-                        nc.tensor.matmul(
-                            pair_sum[k, m][:],
-                            w1_edge[:, d, m * P : (m + 1) * P],
-                            e_sb[k][:, d, :],
-                            start=(d == 0),
-                            stop=False,
-                        )
-                neighbours[k] = held.tile([P, NODES, BLOCKS], BF16, name=f"neighbours_{k}")
-                if k == 0:
-                    for d in range(BLOCKS):
-                        picked = held.tile([P, NODES], F32, name=f"picked_{d}")
-                        nc.scalar.activation(picked[:], x_f32[d][:].indirect(offsets[:, 0 : NODES // 16]), COPY)
-                        nc.vector.tensor_copy(neighbours[k][:, :, d], picked[:])
-                else:
-                    for d in range(BLOCKS):
-                        for piece in range(NODES // PIECE):
-                            first_column = (k * NODES + piece * PIECE) // 16
-                            nc.scalar.activation(
-                                neighbours[k][:, piece * PIECE : (piece + 1) * PIECE, d],
-                                x_bf16[d][:].indirect(offsets[:, first_column : first_column + PIECE // 16]),
-                                COPY,
-                            )
+                    nc.tensor.matmul(
+                        pair_sum[k, m][:], w1_edge[:, d, m * P : (m + 1) * P], e_sb[k][:, d, :], start=(d == 0), stop=False
+                    )
 
-            if step == 1:
+        def own_matmuls():
+            for m in range(BLOCKS):
+                own_sum = msg_banks.tile([P, NODES], F32, name="own_sum", tag=f"msg_sum_{m}")
+                for d in range(BLOCKS):
+                    nc.tensor.matmul(
+                        own_sum[:], w1_self[:, d, m * P : (m + 1) * P], x_bf16[d][:], start=(d == 0), stop=(d == BLOCKS - 1)
+                    )
+                nc.vector.tensor_copy(own_term[m][:], own_sum[:])
+
+        def neighbour_matmuls(k):
+            for d in range(BLOCKS):
                 for m in range(BLOCKS):
-                    own_sum = msg_banks.tile([P, NODES], F32, name="own_sum", tag=f"msg_sum_{m}")
-                    for d in range(BLOCKS):
-                        nc.tensor.matmul(
-                            own_sum[:],
-                            w1_self[:, d, m * P : (m + 1) * P],
-                            x_bf16[d][:],
-                            start=(d == 0),
-                            stop=(d == BLOCKS - 1),
-                        )
-                    nc.vector.tensor_copy(own_term[m][:], own_sum[:])
+                    nc.tensor.matmul(
+                        pair_sum[k, m][:],
+                        w1_neighbour[:, d, m * P : (m + 1) * P],
+                        neighbours[k][:, :, d],
+                        start=False,
+                        stop=(d == BLOCKS - 1),
+                    )
+            for m in range(BLOCKS):
+                before_gelu[k, m] = held.tile([P, NODES], F32, name=f"before_gelu_{k}_{m}")
+                nc.vector.tensor_add(before_gelu[k, m][:], pair_sum[k, m][:], own_term[m][:])
+
+        edge_matmuls(0)
+        edge_matmuls(1)
+        own_matmuls()
+        neighbour_matmuls(0)
+        neighbour_matmuls(1)
+        edge_matmuls(2)
+        edge_matmuls(3)
+        neighbour_matmuls(2)
+        neighbour_matmuls(3)
 
         HALF = NODES // 2
         halves = [slice(h * HALF, (h + 1) * HALF) for h in range(2)]

@@ -26,29 +26,31 @@ def tile_sequencedenoiser_kernel(tc, x, e, w1, b1, w2, b2, offs, out):
         offsets = held.tile([P, EDGES // 16], U16, name="offsets")
         x_f32 = [held.tile([P, NODES], F32, name=f"x_f32_{d}") for d in range(BLOCKS)]
         e_sb = [held.tile([P, BLOCKS, NODES], BF16, name=f"e_sb_{k}") for k in range(GROUPS)]
-        e_groups = [e[:, k * NODES : (k + 1) * NODES].rearrange("(d p) j -> p d j", p=P) for k in range(GROUPS)]
+        e_groups = [e[:, k * NODES : (k + 1) * NODES].rearrange("(p d) j -> p d j", p=P) for k in range(GROUPS)]
         w1_self = held.tile([P, BLOCKS, FEATURES], BF16, name="w1_self")
         w1_edge = held.tile([P, BLOCKS, FEATURES], BF16, name="w1_edge")
         w1_neighbour = held.tile([P, BLOCKS, FEATURES], BF16, name="w1_neighbour")
-        w1_thirds = [w1[t * FEATURES : (t + 1) * FEATURES, :].rearrange("(d p) m -> p d m", p=P) for t in range(3)]
+        w1_thirds = [w1[t * FEATURES : (t + 1) * FEATURES, :].rearrange("(p d) m -> p d m", p=P) for t in range(3)]
         w2_sb = held.tile([P, BLOCKS, FEATURES], BF16, name="w2_sb")
         b1_sb = held.tile([P, BLOCKS], F32, name="b1_sb")
         b2_sb = held.tile([P, BLOCKS], F32, name="b2_sb")
 
+        x_blocks = x.rearrange("(p d) i -> d p i", p=P)
+        out_blocks = out.rearrange("(p c) i -> c p i", p=P)
         nc.sync.dma_start(e_sb[0][:], e_groups[0])
         nc.scalar.dma_start(w1_edge[:], w1_thirds[1])
         nc.sync.dma_start(offsets[:], offs)
-        nc.scalar.dma_start(x_f32[0][:], x[0:P, :])
+        nc.scalar.dma_start(x_f32[0][:], x_blocks[0])
         nc.gpsimd.dma_start(w1_self[:], w1_thirds[0])
-        nc.sync.dma_start(x_f32[1][:], x[P : 2 * P, :])
+        nc.sync.dma_start(x_f32[1][:], x_blocks[1])
         nc.sync.dma_start(e_sb[1][:], e_groups[1])
         nc.sync.dma_start(w1_neighbour[:], w1_thirds[2])
         nc.sync.dma_start(e_sb[2][:], e_groups[2])
         nc.sync.dma_start(e_sb[3][:], e_groups[3])
-        nc.sync.dma_start(w2_sb[:], w2.rearrange("(r p) c -> p r c", p=P))
+        nc.sync.dma_start(w2_sb[:], w2.rearrange("(p r) c -> p r c", p=P))
         with nc.allow_non_contiguous_dma(reason="a bias lands one value to a partition"):
-            nc.gpsimd.dma_start(b1_sb[:], b1.rearrange("(r p) o -> p (r o)", p=P))
-            nc.gpsimd.dma_start(b2_sb[:], b2.rearrange("(r p) o -> p (r o)", p=P))
+            nc.gpsimd.dma_start(b1_sb[:], b1.rearrange("(p r) o -> p (r o)", p=P))
+            nc.gpsimd.dma_start(b2_sb[:], b2.rearrange("(p r) o -> p (r o)", p=P))
 
         table_warmer = held.tile([P, 1], F32, name="table_warmer")
         nc.vector.memset(table_warmer[:], 0.0)
@@ -82,7 +84,7 @@ def tile_sequencedenoiser_kernel(tc, x, e, w1, b1, w2, b2, offs, out):
             for d in range(BLOCKS):
                 for m in range(BLOCKS):
                     nc.tensor.matmul(
-                        pair_sum[k, m][:], w1_edge[:, d, m * P : (m + 1) * P], e_sb[k][:, d, :], start=(d == 0), stop=False
+                        pair_sum[k, m][:], w1_edge[:, d, m::BLOCKS], e_sb[k][:, d, :], start=(d == 0), stop=False
                     )
 
         def own_matmuls():
@@ -90,7 +92,7 @@ def tile_sequencedenoiser_kernel(tc, x, e, w1, b1, w2, b2, offs, out):
                 own_sum = msg_banks.tile([P, NODES], F32, name="own_sum", tag=f"msg_sum_{m}")
                 for d in range(BLOCKS):
                     nc.tensor.matmul(
-                        own_sum[:], w1_self[:, d, m * P : (m + 1) * P], x_bf16[d][:], start=(d == 0), stop=(d == BLOCKS - 1)
+                        own_sum[:], w1_self[:, d, m::BLOCKS], x_bf16[d][:], start=(d == 0), stop=(d == BLOCKS - 1)
                     )
                 nc.vector.tensor_copy(own_term[m][:], own_sum[:])
 
@@ -99,7 +101,7 @@ def tile_sequencedenoiser_kernel(tc, x, e, w1, b1, w2, b2, offs, out):
                 for m in range(BLOCKS):
                     nc.tensor.matmul(
                         pair_sum[k, m][:],
-                        w1_neighbour[:, d, m * P : (m + 1) * P],
+                        w1_neighbour[:, d, m::BLOCKS],
                         neighbours[k][:, :, d],
                         start=False,
                         stop=(d == BLOCKS - 1),
@@ -132,7 +134,7 @@ def tile_sequencedenoiser_kernel(tc, x, e, w1, b1, w2, b2, offs, out):
                 for c in range(BLOCKS):
                     nc.tensor.matmul(
                         early_sum[c][:],
-                        w2_sb[:, m, c * P : (c + 1) * P],
+                        w2_sb[:, m, c::BLOCKS],
                         hid[:],
                         start=(k == 0 and m == 0),
                         stop=(k == 1 and m == BLOCKS - 1),
@@ -152,7 +154,7 @@ def tile_sequencedenoiser_kernel(tc, x, e, w1, b1, w2, b2, offs, out):
             for h in range(2):
                 for c in range(BLOCKS):
                     nc.tensor.matmul(
-                        late_sum[c, h][:], w2_sb[:, m, c * P : (c + 1) * P], hid[:, halves[h]], start=(m == 0), stop=False
+                        late_sum[c, h][:], w2_sb[:, m, c::BLOCKS], hid[:, halves[h]], start=(m == 0), stop=False
                     )
 
         store_queue = [nc.sync, nc.scalar]
@@ -165,9 +167,9 @@ def tile_sequencedenoiser_kernel(tc, x, e, w1, b1, w2, b2, offs, out):
             for c in range(BLOCKS):
                 for m in range(BLOCKS):
                     nc.tensor.matmul(
-                        late_sum[c, h][:], w2_sb[:, m, c * P : (c + 1) * P], last_hid[m][:], start=False, stop=(m == BLOCKS - 1)
+                        late_sum[c, h][:], w2_sb[:, m, c::BLOCKS], last_hid[m][:], start=False, stop=(m == BLOCKS - 1)
                     )
                 nc.vector.scalar_tensor_tensor(
                     result[c][:, halves[h]], late_sum[c, h][:], 1.0 / GROUPS, without_late[c][:, halves[h]], MULT, ADD
                 )
-                store_queue[c].dma_start(out[c * P : (c + 1) * P, halves[h]], result[c][:, halves[h]])
+                store_queue[c].dma_start(out_blocks[c, :, halves[h]], result[c][:, halves[h]])

@@ -41,12 +41,12 @@ def tile_sequencedenoiser_kernel(tc, x, e, w1, b1, w2, b2, offs, out):
         nc.scalar.dma_start(w1_edge[:], w1_thirds[1])
         nc.sync.dma_start(offsets[:], offs)
         nc.scalar.dma_start(x_f32[0][:], x_blocks[0])
-        nc.gpsimd.dma_start(w1_self[:], w1_thirds[0])
+        nc.gpsimd.dma_start(e_sb[3][:], e_groups[3])
         nc.sync.dma_start(x_f32[1][:], x_blocks[1])
+        nc.sync.dma_start(w1_self[:], w1_thirds[0])
         nc.sync.dma_start(e_sb[1][:], e_groups[1])
         nc.sync.dma_start(w1_neighbour[:], w1_thirds[2])
         nc.sync.dma_start(e_sb[2][:], e_groups[2])
-        nc.sync.dma_start(e_sb[3][:], e_groups[3])
         nc.sync.dma_start(w2_sb[:], w2.rearrange("(p r) c -> p r c", p=P))
         with nc.allow_non_contiguous_dma(reason="a bias lands one value to a partition"):
             nc.gpsimd.dma_start(b1_sb[:], b1.rearrange("(p r) o -> p (r o)", p=P))

@@ -20,12 +20,13 @@ def tile_sequencedenoiser_kernel(tc, x, e, w1, b1, w2, b2, offs, out):
     nc = tc.nc
     with (
         tc.tile_pool(name="held", bufs=1) as held,
+        tc.tile_pool(name="edges", bufs=GROUPS - 1) as edges,
         tc.psum_pool(name="pair_banks", bufs=6) as pair_banks,
         tc.psum_pool(name="msg_banks", bufs=1) as msg_banks,
     ):
         offsets = held.tile([P, EDGES // 16], U16, name="offsets")
         x_f32 = [held.tile([P, NODES], F32, name=f"x_f32_{d}") for d in range(BLOCKS)]
-        e_sb = [held.tile([P, BLOCKS, NODES], BF16, name=f"e_sb_{k}") for k in range(GROUPS)]
+        e_sb = [edges.tile([P, BLOCKS, NODES], BF16, name=f"e_sb_{k}", tag="e_sb") for k in range(GROUPS)]
         e_groups = [e[:, k * NODES : (k + 1) * NODES].rearrange("(p d) j -> p d j", p=P) for k in range(GROUPS)]
         w1_self = held.tile([P, BLOCKS, FEATURES], BF16, name="w1_self")
         w1_edge = held.tile([P, BLOCKS, FEATURES], BF16, name="w1_edge")

@@ -39,9 +39,9 @@ def tile_sequencedenoiser_kernel(tc, x, e, w1, b1, w2, b2, offs, out):
         x_blocks = x.rearrange("(p d) i -> d p i", p=P)
         out_blocks = out.rearrange("(p c) i -> c p i", p=P)
         nc.sync.dma_start(e_sb[0][:], e_groups[0])
-        nc.scalar.dma_start(w1_edge[:], w1_thirds[1])
-        nc.sync.dma_start(offsets[:], offs)
         nc.scalar.dma_start(x_f32[0][:], x_blocks[0])
+        nc.sync.dma_start(offsets[:], offs)
+        nc.scalar.dma_start(w1_edge[:], w1_thirds[1])
         nc.gpsimd.dma_start(e_sb[3][:], e_groups[3])
         nc.sync.dma_start(x_f32[1][:], x_blocks[1])
         nc.sync.dma_start(w1_self[:], w1_thirds[0])

import concourse.mybir as mybir

F32, BF16, U16 = mybir.dt.float32, mybir.dt.bfloat16, mybir.dt.uint16
COPY = mybir.ActivationFunctionType.Copy
GELU_TANH = mybir.ActivationFunctionType.Gelu_apprx_tanh
MULT, ADD = mybir.AluOpType.mult, mybir.AluOpType.add

P = 128
FEATURES = 256
NODES = 512
GROUPS = 4
EDGES = GROUPS * NODES
BLOCKS = FEATURES // P
PIECE = 256

FLOPS = 2 * (3 * FEATURES) * FEATURES * EDGES + 2 * FEATURES * FEATURES * EDGES


def tile_sequencedenoiser_kernel(tc, x, e, w1, b1, w2, b2, offs, out):
    nc = tc.nc
    with (
        tc.tile_pool(name="held", bufs=1) as held,
        tc.tile_pool(name="edges", bufs=GROUPS - 1) as edges,
        tc.psum_pool(name="pair_banks", bufs=6) as pair_banks,
        tc.psum_pool(name="msg_banks", bufs=1) as msg_banks,
    ):
        offsets = held.tile([P, EDGES // 16], U16, name="offsets")
        x_f32 = [held.tile([P, NODES], F32, name=f"x_f32_{d}") for d in range(BLOCKS)]
        e_sb = [edges.tile([P, BLOCKS, NODES], BF16, name=f"e_sb_{k}", tag="e_sb") for k in range(GROUPS)]
        e_groups = [e[:, k * NODES : (k + 1) * NODES].rearrange("(p d) j -> p d j", p=P) for k in range(GROUPS)]
        w1_self = held.tile([P, BLOCKS, FEATURES], BF16, name="w1_self")
        w1_edge = held.tile([P, BLOCKS, FEATURES], BF16, name="w1_edge")
        w1_neighbour = held.tile([P, BLOCKS, FEATURES], BF16, name="w1_neighbour")
        w1_thirds = [w1[t * FEATURES : (t + 1) * FEATURES, :].rearrange("(p d) m -> p d m", p=P) for t in range(3)]
        w2_sb = held.tile([P, BLOCKS, FEATURES], BF16, name="w2_sb")
        b1_sb = held.tile([P, BLOCKS], F32, name="b1_sb")
        b2_sb = held.tile([P, BLOCKS], F32, name="b2_sb")

        x_blocks = x.rearrange("(p d) i -> d p i", p=P)
        out_blocks = out.rearrange("(p c) i -> c p i", p=P)
        nc.sync.dma_start(e_sb[0][:], e_groups[0])
        nc.scalar.dma_start(x_f32[0][:], x_blocks[0])
        nc.sync.dma_start(offsets[:], offs)
        nc.scalar.dma_start(w1_edge[:], w1_thirds[1])
        nc.gpsimd.dma_start(e_sb[3][:], e_groups[3])
        nc.sync.dma_start(x_f32[1][:], x_blocks[1])
        nc.sync.dma_start(w1_self[:], w1_thirds[0])
        nc.sync.dma_start(e_sb[1][:], e_groups[1])
        nc.sync.dma_start(w1_neighbour[:], w1_thirds[2])
        nc.sync.dma_start(e_sb[2][:], e_groups[2])
        nc.sync.dma_start(w2_sb[:], w2.rearrange("(p r) c -> p r c", p=P))
        with nc.allow_non_contiguous_dma(reason="a bias lands one value to a partition"):
            nc.gpsimd.dma_start(b1_sb[:], b1.rearrange("(p r) o -> p (r o)", p=P))
            nc.gpsimd.dma_start(b2_sb[:], b2.rearrange("(p r) o -> p (r o)", p=P))

        table_warmer = held.tile([P, 1], F32, name="table_warmer")
        nc.vector.memset(table_warmer[:], 0.0)
        nc.scalar.activation(table_warmer[:], table_warmer[:], GELU_TANH)

        x_bf16 = [held.tile([P, NODES], BF16, name=f"x_bf16_{d}") for d in range(BLOCKS)]
        for d in range(BLOCKS):
            nc.vector.tensor_copy(x_bf16[d][:], x_f32[d][:])
        neighbours = [held.tile([P, NODES, BLOCKS], BF16, name=f"neighbours_{k}") for k in range(GROUPS)]
        for d in range(BLOCKS):
            picked = held.tile([P, NODES], F32, name=f"picked_{d}")
            nc.scalar.activation(picked[:], x_f32[d][:].indirect(offsets[:, 0 : NODES // 16]), COPY)
            nc.vector.tensor_copy(neighbours[0][:, :, d], picked[:])
        for k in range(1, GROUPS):
            for d in range(BLOCKS):
                for piece in range(NODES // PIECE):
                    first_column = (k * NODES + piece * PIECE) // 16
                    nc.scalar.activation(
                        neighbours[k][:, piece * PIECE : (piece + 1) * PIECE, d],
                        x_bf16[d][:].indirect(offsets[:, first_column : first_column + PIECE // 16]),
                        COPY,
                    )

        own_term = [held.tile([P, NODES], F32, name=f"own_term_{m}") for m in range(BLOCKS)]
        pair_sum = {}
        before_gelu = {}

        def edge_matmuls(k):
            for m in range(BLOCKS):
                pair_sum[k, m] = pair_banks.tile([P, NODES], F32, name="pair_sum")
            for d in range(BLOCKS):
                for m in range(BLOCKS):
                    nc.tensor.matmul(
                        pair_sum[k, m][:], w1_edge[:, d, m::BLOCKS], e_sb[k][:, d, :], start=(d == 0), stop=False
                    )

        def own_matmuls():
            for m in range(BLOCKS):
                own_sum = msg_banks.tile([P, NODES], F32, name="own_sum", tag=f"msg_sum_{m}")
                for d in range(BLOCKS):
                    nc.tensor.matmul(
                        own_sum[:], w1_self[:, d, m::BLOCKS], x_bf16[d][:], start=(d == 0), stop=(d == BLOCKS - 1)
                    )
                nc.vector.tensor_copy(own_term[m][:], own_sum[:])

        def neighbour_matmuls(k):
            for d in range(BLOCKS):
                for m in range(BLOCKS):
                    nc.tensor.matmul(
                        pair_sum[k, m][:],
                        w1_neighbour[:, d, m::BLOCKS],
                        neighbours[k][:, :, d],
                        start=False,
                        stop=(d == BLOCKS - 1),
                    )
            for m in range(BLOCKS):
                before_gelu[k, m] = held.tile([P, NODES], F32, name=f"before_gelu_{k}_{m}")
                nc.vector.tensor_add(before_gelu[k, m][:], pair_sum[k, m][:], own_term[m][:])

        edge_matmuls(0)
        edge_matmuls(1)
        own_matmuls()
        neighbour_matmuls(0)
        neighbour_matmuls(1)
        edge_matmuls(2)
        edge_matmuls(3)
        neighbour_matmuls(2)
        neighbour_matmuls(3)

        HALF = NODES // 2
        halves = [slice(h * HALF, (h + 1) * HALF) for h in range(2)]
        x_plus_b2 = [held.tile([P, NODES], F32, name=f"x_plus_b2_{c}") for c in range(BLOCKS)]
        for c in range(BLOCKS):
            nc.vector.tensor_scalar_add(x_plus_b2[c][:], x_f32[c][:], b2_sb[:, c : c + 1])

        early_sum = [msg_banks.tile([P, NODES], F32, name=f"msg_sum_{c}") for c in range(BLOCKS)]
        for k in range(2):
            for m in range(BLOCKS):
                hid = held.tile([P, NODES], BF16, name=f"hid_{k}_{m}")
                nc.scalar.activation(hid[:], before_gelu[k, m][:], GELU_TANH, bias=b1_sb[:, m : m + 1])
                for c in range(BLOCKS):
                    nc.tensor.matmul(
                        early_sum[c][:],
                        w2_sb[:, m, c::BLOCKS],
                        hid[:],
                        start=(k == 0 and m == 0),
                        stop=(k == 1 and m == BLOCKS - 1),
                    )
        without_late = [held.tile([P, NODES], F32, name=f"without_late_{c}") for c in range(BLOCKS)]
        for c in range(BLOCKS):
            nc.vector.scalar_tensor_tensor(without_late[c][:], early_sum[c][:], 1.0 / GROUPS, x_plus_b2[c][:], MULT, ADD)

        late_sum = {
            (c, h): pair_banks.tile([P, HALF], F32, name=f"late_sum_{c}_{h}", tag="pair_sum")
            for h in range(2)
            for c in range(BLOCKS)
        }
        for m in range(BLOCKS):
            hid = held.tile([P, NODES], BF16, name=f"hid_2_{m}")
            nc.scalar.activation(hid[:], before_gelu[2, m][:], GELU_TANH, bias=b1_sb[:, m : m + 1])
            for h in range(2):
                for c in range(BLOCKS):
                    nc.tensor.matmul(
                        late_sum[c, h][:], w2_sb[:, m, c::BLOCKS], hid[:, halves[h]], start=(m == 0), stop=False
                    )

        store_queue = [nc.sync, nc.scalar]
        result = [held.tile([P, NODES], F32, name=f"result_{c}") for c in range(BLOCKS)]
        for h in range(2):
            last_hid = []
            for m in range(BLOCKS):
                last_hid.append(held.tile([P, HALF], BF16, name=f"hid_3_{m}_{h}"))
                nc.scalar.activation(last_hid[m][:], before_gelu[3, m][:, halves[h]], GELU_TANH, bias=b1_sb[:, m : m + 1])
            for c in range(BLOCKS):
                for m in range(BLOCKS):
                    nc.tensor.matmul(
                        late_sum[c, h][:], w2_sb[:, m, c::BLOCKS], last_hid[m][:], start=False, stop=(m == BLOCKS - 1)
                    )
                nc.vector.scalar_tensor_tensor(
                    result[c][:, halves[h]], late_sum[c, h][:], 1.0 / GROUPS, without_late[c][:, halves[h]], MULT, ADD
                )
                store_queue[c].dma_start(out_blocks[c, :, halves[h]], result[c][:, halves[h]])
